import numpy as np
import ml_dtypes


def mxq(x, axis, fmt="e4m3"):
    dtype, down = {"e4m3": (ml_dtypes.float8_e4m3fn, 7), "e5m2": (ml_dtypes.float8_e5m2, 14)}[fmt]
    v = np.moveaxis(np.asarray(x, np.float32).astype(ml_dtypes.bfloat16).astype(np.float64), axis, -1)
    blocks = v.reshape(v.shape[:-1] + (-1, 32))
    amax = np.abs(blocks).max(-1, keepdims=True)
    byte = np.maximum(np.where(amax > 0, np.frexp(amax)[1] - 1 + 127, 0) - down, 1)
    scale = np.exp2(byte - 127.0)
    codes = (blocks / scale).astype(np.float32).astype(dtype).astype(np.float64)
    return np.moveaxis((codes * scale).reshape(v.shape), -1, axis)


WIDE = False


def mx_kscale(k):
    if not WIDE:
        return np.ones(k)
    levels = np.array([20, -20, 10, -10, 0])
    a = np.random.permutation(np.resize(levels, k // 512 * 4)).reshape(k // 512, 4)
    idx = np.arange(k)
    return np.exp2(a[idx // 512, idx % 128 // 32])


BF16 = ml_dtypes.bfloat16


def bf(x):
    return np.asarray(x, np.float32).astype(BF16)


def f64(x):
    return np.asarray(x).astype(np.float64)


B, NB, IBS, BS = 512, 4, 512, 512


def sigmoid(v):
    return 1.0 / (1.0 + np.exp(-v))


def gru_parts(x, h, W_ih, W_hh, b_ih, b_hh):
    xb = f64(x).reshape(B, NB, IBS)
    hb = f64(h).reshape(B, NB, BS)
    gi = (xb.transpose(1, 0, 2) @ f64(W_ih).transpose(0, 2, 1)).transpose(1, 0, 2) + f64(b_ih)
    gh = (hb.transpose(1, 0, 2) @ f64(W_hh).transpose(0, 2, 1)).transpose(1, 0, 2) + f64(b_hh)
    i_r, i_z, i_n = np.split(gi, 3, axis=-1)
    h_r, h_z, hn = np.split(gh, 3, axis=-1)
    r = sigmoid(i_r + h_r)
    z = sigmoid(i_z + h_z)
    c = np.tanh(i_n + r * hn)
    return r, z, c, hn, hb


def setup_inputs():
    u = mx_kscale(BS)
    x = bf(np.random.standard_normal((B, NB, IBS)).reshape(B, NB * IBS))
    h = bf(np.random.standard_normal((B, NB * BS)))
    W0 = bf(np.random.standard_normal((NB, 3 * BS, IBS)) / np.sqrt(IBS))
    W_hh = bf(np.random.standard_normal((NB, 3 * BS, BS)) / np.sqrt(BS))
    b_ih = bf(np.random.standard_normal((NB, 3 * BS)) * 0.2)
    b_hh = bf(np.random.standard_normal((NB, 3 * BS)) * 0.2)
    g = bf((np.random.standard_normal((B, NB, BS)) * np.exp2(np.random.randint(-12, 1, (B, 1, 1))) * 16.0 * u).reshape(B, NB * BS))
    r, z, c, hn, _ = gru_parts(x, h, W0, W_hh, b_ih, b_hh)
    gates = np.concatenate([r, z, c], axis=-1)
    W_ih = bf(f64(W0) / np.tile(u, 3)[None, :, None])
    return {
        "x": x,
        "h": h,
        "W_ih": W_ih,
        "W_hh": W_hh,
        "b_ih": b_ih,
        "b_hh": b_hh,
        "gates": np.asarray(gates, np.float32),
        "h_n": np.asarray(hn, np.float32),
        "grad_out": g,
    }


def reference(x, h, W_ih, W_hh, b_ih, b_hh, gates, h_n, grad_out):
    g = f64(grad_out).reshape(B, NB, BS)
    hb = f64(h).reshape(B, NB, BS)
    r, z, c = np.split(f64(gates), 3, axis=-1)
    hn = f64(h_n)
    d_n = g * (1.0 - z) * (1.0 - c * c)
    d_r = d_n * hn * r * (1.0 - r)
    d_z = g * (hb - c) * z * (1.0 - z)
    dgi = np.concatenate([d_r, d_z, d_n], axis=-1)
    dx = mxq(dgi, 2, "e5m2").transpose(1, 0, 2) @ mxq(f64(W_ih), 1, "e4m3")
    return dx.transpose(1, 0, 2).reshape(B, NB * IBS)

@@ -1,0 +1,245 @@
+from contextlib import ExitStack
+
+import concourse.mybir as mybir
+from concourse.masks import make_identity
+
+F32 = mybir.dt.float32
+BF16 = mybir.dt.bfloat16
+U32 = mybir.dt.uint32
+U8 = mybir.dt.uint8
+E4M3_X4 = mybir.dt.float8_e4m3fn_x4
+E5M2_X4 = mybir.dt.float8_e5m2_x4
+ALU = mybir.AluOpType
+ACT = mybir.ActivationFunctionType
+
+P = 128
+PACK = 4
+BATCH = 512
+BLOCKS = 4
+BLOCK = 512
+PARTS = 3
+ROW_TILES = BATCH // P
+R, Z, N = 0, 1, 2
+GATE_R, GATE_Z, GATE_C = 0, 1, 2
+
+LOAD_AHEAD = 5
+
+FLOPS = 2 * BATCH * BLOCKS * PARTS * BLOCK * BLOCK
+BYTES = BATCH * BLOCKS * BLOCK * (PARTS * 4 + 4 + 2 + 2 + 4) + BLOCKS * PARTS * BLOCK * BLOCK * 2
+
+
+def tile_blockdiagonalgru_v_kernel(tc, x, h, W_ih, W_hh, b_ih, b_hh, gates, h_n, grad_out, out):
+    nc = tc.nc
+    chunks = [(n, i) for n in range(BLOCKS) for i in range(ROW_TILES)]
+    steps = len(chunks)
+
+    with ExitStack() as ctx:
+        keep = ctx.enter_context(tc.tile_pool(name="keep", bufs=1))
+        loads = ctx.enter_context(tc.tile_pool(name="loads", bufs=LOAD_AHEAD))
+        w_raws = ctx.enter_context(tc.tile_pool(name="w_raws", bufs=4))
+        pairs = ctx.enter_context(tc.tile_pool(name="pairs", bufs=2))
+        results = ctx.enter_context(tc.tile_pool(name="results", bufs=3))
+        banks = ctx.enter_context(tc.psum_pool(name="banks", bufs=1))
+        sums = ctx.enter_context(tc.psum_pool(name="sums", bufs=2))
+        ctx.enter_context(tc.manual_schedule())
+
+        ident_f32 = keep.tile([P, P], F32)
+        make_identity(nc, ident_f32[:])
+        ident_bf16 = keep.tile([P, P], BF16)
+        make_identity(nc, ident_bf16[:])
+        w_codes = keep.tile([P, BLOCKS, PARTS, BLOCK], U32, align_bytes=64)
+        w_scales = keep.tile([P, BLOCKS, PARTS, BLOCK], U8, align_bytes=64)
+
+        loaded = {}
+        factors = {}
+        turned = {}
+        rounded = {}
+        w_raw_of = {}
+        w_grouped_of = {}
+
+        def weights_of_step(step):
+            n, a = step // ROW_TILES + 1, step % ROW_TILES
+            return (n, a) if (step >= 0 and n < BLOCKS and a < PARTS) else None
+
+        def load_weights(which):
+            n, a = which
+            w_raw = w_raws.tile([P, PACK, BLOCK], BF16)
+            rows = W_ih[n, a * BLOCK : (a + 1) * BLOCK, :]
+            nc.sync.dma_start(out=w_raw[:], in_=rows.rearrange("(t p) j -> p t j", p=P))
+            w_raw_of[which] = w_raw
+
+        def regroup_weights(which):
+            w_grouped = pairs.tile([P, BLOCK, PACK], BF16, align_bytes=64)
+            nc.scalar.copy(
+                out=w_grouped[:].rearrange("p (c i) t -> p c t i", i=4),
+                in_=w_raw_of[which][:].rearrange("p t (c i) -> p c t i", i=4),
+            )
+            w_grouped_of[which] = w_grouped
+
+        def quantise_weights(which):
+            n, a = which
+            nc.vector.quantize_mx(
+                out=w_codes[:, n, a, :].bitcast(E4M3_X4),
+                scales=w_scales[:, n, a, :],
+                in_=w_grouped_of[which][:].rearrange("p j t -> p (j t)"),
+            )
+
+        def load_chunk(j):
+            n, i = chunks[j]
+            rows = slice(i * P, (i + 1) * P)
+            cols = slice(n * BLOCK, (n + 1) * BLOCK)
+            g_in = loads.tile([P, BLOCK], BF16)
+            nc.sync.dma_start(out=g_in[:], in_=grad_out[rows, cols])
+            gates_in = loads.tile([P, PARTS, BLOCK], F32)
+            nc.sync.dma_start(out=gates_in[:], in_=gates[rows, n, :].rearrange("b (a k) -> b a k", a=PARTS))
+            h_in = loads.tile([P, BLOCK], BF16)
+            nc.sync.dma_start(out=h_in[:], in_=h[rows, cols])
+            hn_in = loads.tile([P, BLOCK], F32)
+            nc.sync.dma_start(out=hn_in[:], in_=h_n[rows, n, :])
+            loaded[j] = (g_in, gates_in, h_in, hn_in)
+
+        def stream_in(j):
+            if weights_of_step(j - 2) is not None:
+                load_weights(weights_of_step(j - 2))
+            if j < steps:
+                load_chunk(j)
+
+        def make_factors(j):
+            if j >= steps:
+                return
+            g_in, gates_in, h_in, hn_in = loaded[j]
+            c_sq = pairs.tile([P, BLOCK], F32)
+            nc.scalar.activation(out=c_sq[:], in_=gates_in[:, GATE_C, :], func=ACT.Square)
+            r_hn = pairs.tile([P, BLOCK], F32)
+            nc.gpsimd.tensor_tensor(out=r_hn[:], in0=gates_in[:, GATE_R, :], in1=hn_in[:], op=ALU.mult)
+            c_minus_h = pairs.tile([P, BLOCK], F32)
+            nc.gpsimd.tensor_tensor(out=c_minus_h[:], in0=gates_in[:, GATE_C, :], in1=h_in[:], op=ALU.subtract)
+            factors[j] = (c_sq, c_minus_h, r_hn)
+
+        def turn(j, name, plane, identity):
+            bank = banks.tile([P, PACK, P], plane.dtype, name=name)
+            for t in range(PACK):
+                nc.tensor.transpose(out=bank[:, t, :], in_=plane[:, t * P : (t + 1) * P], identity=identity[:])
+            turned[(j, name)] = bank
+
+        def words(j, name):
+            return turned[(j, name)][:].rearrange("p t b -> p b t")
+
+        def turn_g(j):
+            if j >= steps:
+                return
+            turn(j, "g_bank", loaded[j][0], ident_bf16)
+            g_t = pairs.tile([P, P, PACK], BF16)
+            nc.scalar.copy(out=g_t[:], in_=words(j, "g_bank"))
+            turned[(j, "g")] = g_t
+
+        def quantise(j):
+            dgi = rounded[j]
+            d_codes = pairs.tile([P, PARTS, P], U32, align_bytes=64)
+            d_scales = pairs.tile([P, PARTS, P], U8, align_bytes=64)
+            nc.vector.quantize_mx(
+                out=d_codes[:, R : Z + 1, :].rearrange("p a b -> p (a b)").bitcast(E5M2_X4),
+                scales=d_scales[:, R : Z + 1, :].rearrange("p a b -> p (a b)"),
+                in_=dgi[:, R : Z + 1].rearrange("p a b t -> p (a b t)"),
+            )
+            nc.vector.quantize_mx(
+                out=d_codes[:, N, :].bitcast(E5M2_X4),
+                scales=d_scales[:, N, :],
+                in_=dgi[:, N].rearrange("p b t -> p (b t)"),
+            )
+            return d_codes, d_scales
+
+        def multiply(j, d_codes, d_scales):
+            n, i = chunks[j]
+            acc = sums.tile([P, BLOCK], F32)
+            for a in range(PARTS):
+                nc.tensor.matmul_mx(
+                    out=acc[:],
+                    lhsT=d_codes[:, a, :].bitcast(E5M2_X4),
+                    lhsT_scale=d_scales[:, a, :],
+                    rhs=w_codes[:, n, a, :].bitcast(E4M3_X4),
+                    rhs_scale=w_scales[:, n, a, :],
+                    start=(a == 0),
+                    stop=(a == PARTS - 1),
+                )
+            return acc
+
+        def store(j, acc):
+            n, i = chunks[j]
+            result = results.tile([P, BLOCK], F32)
+            nc.scalar.copy(out=result[:], in_=acc[:])
+            nc.scalar.dma_start(out=out[i * P : (i + 1) * P, n * BLOCK : (n + 1) * BLOCK], in_=result[:])
+
+        for a in range(PARTS):
+            load_weights((0, a))
+        for j in range(LOAD_AHEAD):
+            stream_in(j)
+        regroup_weights((0, 0))
+        regroup_weights((0, 1))
+        quantise_weights((0, 0))
+        regroup_weights((0, 2))
+        quantise_weights((0, 1))
+        quantise_weights((0, 2))
+        make_factors(0)
+        turn_g(0)
+        turn(0, "c_sq", factors[0][0], ident_f32)
+        turn(0, "z", loaded[0][1][:, GATE_Z, :], ident_f32)
+        turn(0, "r_hn", factors[0][2], ident_f32)
+        turn(0, "c_minus_h", factors[0][1], ident_f32)
+        turn(0, "r", loaded[0][1][:, GATE_R, :], ident_f32)
+        make_factors(1)
+
+        for j in range(steps + 1):
+            nxt = j + 1
+            stream_in(j + LOAD_AHEAD)
+            turn_g(nxt)
+            if j < steps:
+                dgi = pairs.tile([P, PARTS, P, PACK], BF16, align_bytes=64)
+                rounded[j] = dgi
+                z_words = words(j, "z")
+                minus_a = pairs.tile([P, P, PACK], F32)
+                nc.vector.scalar_tensor_tensor(
+                    out=minus_a[:], in0=z_words, scalar=1.0, in1=turned[(j, "g")][:],
+                    op0=ALU.subtract, op1=ALU.mult,
+                )
+            if j > 0:
+                d_codes, d_scales = quantise(j - 1)
+                if weights_of_step(j - 1) is not None:
+                    quantise_weights(weights_of_step(j - 1))
+                acc = multiply(j - 1, d_codes, d_scales)
+            if j < steps:
+                d_n = pairs.tile([P, P, PACK], F32)
+                nc.vector.scalar_tensor_tensor(
+                    out=d_n[:], in0=words(j, "c_sq"), scalar=1.0, in1=minus_a[:],
+                    op0=ALU.subtract, op1=ALU.mult,
+                )
+                if nxt < steps:
+                    turn(nxt, "c_sq", factors[nxt][0], ident_f32)
+                nc.gpsimd.tensor_scalar(
+                    out=dgi[:, N], in0=d_n[:], scalar1=1.0, scalar2=0.0, op0=ALU.mult, op1=ALU.add
+                )
+                minus_az = pairs.tile([P, P, PACK], F32)
+                nc.vector.tensor_tensor(out=minus_az[:], in0=z_words, in1=minus_a[:], op=ALU.mult)
+                if nxt < steps:
+                    turn(nxt, "z", loaded[nxt][1][:, GATE_Z, :], ident_f32)
+                minus_dn_r_hn = pairs.tile([P, P, PACK], F32)
+                nc.vector.scalar_tensor_tensor(
+                    out=minus_dn_r_hn[:], in0=words(j, "r_hn"), scalar=-1.0, in1=d_n[:],
+                    op0=ALU.mult, op1=ALU.mult,
+                )
+                if nxt < steps:
+                    turn(nxt, "r_hn", factors[nxt][2], ident_f32)
+                nc.vector.tensor_tensor(out=dgi[:, Z], in0=words(j, "c_minus_h"), in1=minus_az[:], op=ALU.mult)
+                if nxt < steps:
+                    turn(nxt, "c_minus_h", factors[nxt][1], ident_f32)
+                nc.vector.scalar_tensor_tensor(
+                    out=dgi[:, R], in0=words(j, "r"), scalar=1.0, in1=minus_dn_r_hn[:],
+                    op0=ALU.subtract, op1=ALU.mult,
+                )
+                if nxt < steps:
+                    turn(nxt, "r", loaded[nxt][1][:, GATE_R, :], ident_f32)
+            if weights_of_step(j) is not None:
+                regroup_weights(weights_of_step(j))
+            if j > 0:
+                store(j - 1, acc)
+            make_factors(j + 2)

@@ -47,6 +47,8 @@ def tile_blockdiagonalgru_v_kernel(tc, x, h, W_ih, W_hh, b_ih, b_hh, gates, h_n,
         make_identity(nc, ident_f32[:])
         ident_bf16 = keep.tile([P, P], BF16)
         make_identity(nc, ident_bf16[:])
+        minus_ident_bf16 = keep.tile([P, P], BF16)
+        nc.vector.tensor_scalar_mul(out=minus_ident_bf16[:], in0=ident_bf16[:], scalar1=-1.0)
         w_codes = keep.tile([P, BLOCKS, PARTS, BLOCK], U32, align_bytes=64)
         w_scales = keep.tile([P, BLOCKS, PARTS, BLOCK], U8, align_bytes=64)
 
@@ -112,15 +114,27 @@ def tile_blockdiagonalgru_v_kernel(tc, x, h, W_ih, W_hh, b_ih, b_hh, gates, h_n,
             nc.scalar.activation(out=c_sq[:], in_=gates_in[:, GATE_C, :], func=ACT.Square)
             r_hn = pairs.tile([P, BLOCK], F32)
             nc.gpsimd.tensor_tensor(out=r_hn[:], in0=gates_in[:, GATE_R, :], in1=hn_in[:], op=ALU.mult)
-            c_minus_h = pairs.tile([P, BLOCK], F32)
-            nc.gpsimd.tensor_tensor(out=c_minus_h[:], in0=gates_in[:, GATE_C, :], in1=h_in[:], op=ALU.subtract)
-            factors[j] = (c_sq, c_minus_h, r_hn)
+            factors[j] = (c_sq, r_hn)
 
         def turn(j, name, plane, identity):
             bank = banks.tile([P, PACK, P], plane.dtype, name=name)
             for t in range(PACK):
                 nc.tensor.transpose(out=bank[:, t, :], in_=plane[:, t * P : (t + 1) * P], identity=identity[:])
             turned[(j, name)] = bank
+
+        def turn_c_minus_h(j):
+            g_in, gates_in, h_in, hn_in = loaded[j]
+            bank = banks.tile([P, PACK, P], F32, name="c_minus_h")
+            for t in range(PACK):
+                k = slice(t * P, (t + 1) * P)
+                nc.tensor.matmul(
+                    out=bank[:, t, :], lhsT=gates_in[:, GATE_C, k], rhs=ident_f32[:],
+                    is_transpose=True, start=True, stop=False,
+                )
+                nc.tensor.matmul(
+                    out=bank[:, t, :], lhsT=h_in[:, k], rhs=minus_ident_bf16[:], start=False, stop=True
+                )
+            turned[(j, "c_minus_h")] = bank
 
         def words(j, name):
             return turned[(j, name)][:].rearrange("p t b -> p b t")
@@ -184,8 +198,8 @@ def tile_blockdiagonalgru_v_kernel(tc, x, h, W_ih, W_hh, b_ih, b_hh, gates, h_n,
         turn_g(0)
         turn(0, "c_sq", factors[0][0], ident_f32)
         turn(0, "z", loaded[0][1][:, GATE_Z, :], ident_f32)
-        turn(0, "r_hn", factors[0][2], ident_f32)
-        turn(0, "c_minus_h", factors[0][1], ident_f32)
+        turn(0, "r_hn", factors[0][1], ident_f32)
+        turn_c_minus_h(0)
         turn(0, "r", loaded[0][1][:, GATE_R, :], ident_f32)
         make_factors(1)
 
@@ -228,10 +242,10 @@ def tile_blockdiagonalgru_v_kernel(tc, x, h, W_ih, W_hh, b_ih, b_hh, gates, h_n,
                     op0=ALU.mult, op1=ALU.mult,
                 )
                 if nxt < steps:
-                    turn(nxt, "r_hn", factors[nxt][2], ident_f32)
+                    turn(nxt, "r_hn", factors[nxt][1], ident_f32)
                 nc.vector.tensor_tensor(out=dgi[:, Z], in0=words(j, "c_minus_h"), in1=minus_az[:], op=ALU.mult)
                 if nxt < steps:
-                    turn(nxt, "c_minus_h", factors[nxt][1], ident_f32)
+                    turn_c_minus_h(nxt)
                 nc.vector.scalar_tensor_tensor(
                     out=dgi[:, R], in0=words(j, "r"), scalar=1.0, in1=minus_dn_r_hn[:],
                     op0=ALU.subtract, op1=ALU.mult,

@@ -38,7 +38,7 @@ def tile_blockdiagonalgru_v_kernel(tc, x, h, W_ih, W_hh, b_ih, b_hh, gates, h_n,
         loads = ctx.enter_context(tc.tile_pool(name="loads", bufs=LOAD_AHEAD))
         w_raws = ctx.enter_context(tc.tile_pool(name="w_raws", bufs=4))
         pairs = ctx.enter_context(tc.tile_pool(name="pairs", bufs=2))
-        results = ctx.enter_context(tc.tile_pool(name="results", bufs=3))
+        w_groups = ctx.enter_context(tc.tile_pool(name="w_groups", bufs=PARTS))
         banks = ctx.enter_context(tc.psum_pool(name="banks", bufs=1))
         sums = ctx.enter_context(tc.psum_pool(name="sums", bufs=2))
         ctx.enter_context(tc.manual_schedule())
@@ -51,6 +51,7 @@ def tile_blockdiagonalgru_v_kernel(tc, x, h, W_ih, W_hh, b_ih, b_hh, gates, h_n,
         nc.vector.tensor_scalar_mul(out=minus_ident_bf16[:], in0=ident_bf16[:], scalar1=-1.0)
         w_codes = keep.tile([P, BLOCKS, PARTS, BLOCK], U32, align_bytes=64)
         w_scales = keep.tile([P, BLOCKS, PARTS, BLOCK], U8, align_bytes=64)
+        results = keep.tile([P, steps, BLOCK], F32)
 
         loaded = {}
         factors = {}
@@ -60,8 +61,10 @@ def tile_blockdiagonalgru_v_kernel(tc, x, h, W_ih, W_hh, b_ih, b_hh, gates, h_n,
         w_grouped_of = {}
 
         def weights_of_step(step):
+            if step == -1:
+                return [(0, a) for a in range(PARTS)]
             n, a = step // ROW_TILES + 1, step % ROW_TILES
-            return (n, a) if (step >= 0 and n < BLOCKS and a < PARTS) else None
+            return [(n, a)] if (step >= 0 and n < BLOCKS and a < PARTS) else []
 
         def load_weights(which):
             n, a = which
@@ -71,7 +74,7 @@ def tile_blockdiagonalgru_v_kernel(tc, x, h, W_ih, W_hh, b_ih, b_hh, gates, h_n,
             w_raw_of[which] = w_raw
 
         def regroup_weights(which):
-            w_grouped = pairs.tile([P, BLOCK, PACK], BF16, align_bytes=64)
+            w_grouped = w_groups.tile([P, BLOCK, PACK], BF16, align_bytes=64)
             nc.scalar.copy(
                 out=w_grouped[:].rearrange("p (c i) t -> p c t i", i=4),
                 in_=w_raw_of[which][:].rearrange("p t (c i) -> p c t i", i=4),
@@ -101,8 +104,8 @@ def tile_blockdiagonalgru_v_kernel(tc, x, h, W_ih, W_hh, b_ih, b_hh, gates, h_n,
             loaded[j] = (g_in, gates_in, h_in, hn_in)
 
         def stream_in(j):
-            if weights_of_step(j - 2) is not None:
-                load_weights(weights_of_step(j - 2))
+            for which in weights_of_step(j - 2):
+                load_weights(which)
             if j < steps:
                 load_chunk(j)
 
@@ -178,22 +181,12 @@ def tile_blockdiagonalgru_v_kernel(tc, x, h, W_ih, W_hh, b_ih, b_hh, gates, h_n,
                 )
             return acc
 
-        def store(j, acc):
+        def store(j):
             n, i = chunks[j]
-            result = results.tile([P, BLOCK], F32)
-            nc.scalar.copy(out=result[:], in_=acc[:])
-            nc.scalar.dma_start(out=out[i * P : (i + 1) * P, n * BLOCK : (n + 1) * BLOCK], in_=result[:])
+            nc.sync.dma_start(out=out[i * P : (i + 1) * P, n * BLOCK : (n + 1) * BLOCK], in_=results[:, j, :])
 
-        for a in range(PARTS):
-            load_weights((0, a))
         for j in range(LOAD_AHEAD):
             stream_in(j)
-        regroup_weights((0, 0))
-        regroup_weights((0, 1))
-        quantise_weights((0, 0))
-        regroup_weights((0, 2))
-        quantise_weights((0, 1))
-        quantise_weights((0, 2))
         make_factors(0)
         turn_g(0)
         turn(0, "c_sq", factors[0][0], ident_f32)
@@ -201,8 +194,11 @@ def tile_blockdiagonalgru_v_kernel(tc, x, h, W_ih, W_hh, b_ih, b_hh, gates, h_n,
         turn(0, "r_hn", factors[0][1], ident_f32)
         turn_c_minus_h(0)
         turn(0, "r", loaded[0][1][:, GATE_R, :], ident_f32)
+        for which in weights_of_step(-1):
+            regroup_weights(which)
         make_factors(1)
 
+        first_step_without_loads = steps - LOAD_AHEAD
         for j in range(steps + 1):
             nxt = j + 1
             stream_in(j + LOAD_AHEAD)
@@ -218,8 +214,8 @@ def tile_blockdiagonalgru_v_kernel(tc, x, h, W_ih, W_hh, b_ih, b_hh, gates, h_n,
                 )
             if j > 0:
                 d_codes, d_scales = quantise(j - 1)
-                if weights_of_step(j - 1) is not None:
-                    quantise_weights(weights_of_step(j - 1))
+                for which in weights_of_step(j - 2):
+                    quantise_weights(which)
                 acc = multiply(j - 1, d_codes, d_scales)
             if j < steps:
                 d_n = pairs.tile([P, P, PACK], F32)
@@ -252,8 +248,13 @@ def tile_blockdiagonalgru_v_kernel(tc, x, h, W_ih, W_hh, b_ih, b_hh, gates, h_n,
                 )
                 if nxt < steps:
                     turn(nxt, "r", loaded[nxt][1][:, GATE_R, :], ident_f32)
-            if weights_of_step(j) is not None:
-                regroup_weights(weights_of_step(j))
+            for which in weights_of_step(j):
+                regroup_weights(which)
             if j > 0:
-                store(j - 1, acc)
+                nc.scalar.copy(out=results[:, j - 1, :], in_=acc[:])
+            if j == first_step_without_loads:
+                for finished in range(j - 1):
+                    store(finished)
+            if j >= first_step_without_loads:
+                store(j - 1)
             make_factors(j + 2)

@@ -166,10 +166,9 @@ def tile_blockdiagonalgru_v_kernel(tc, x, h, W_ih, W_hh, b_ih, b_hh, gates, h_n,
             )
             return d_codes, d_scales
 
-        def multiply(j, d_codes, d_scales):
+        def multiply(j, acc, d_codes, d_scales, parts):
             n, i = chunks[j]
-            acc = sums.tile([P, BLOCK], F32)
-            for a in range(PARTS):
+            for a in parts:
                 nc.tensor.matmul_mx(
                     out=acc[:],
                     lhsT=d_codes[:, a, :].bitcast(E5M2_X4),
@@ -179,7 +178,6 @@ def tile_blockdiagonalgru_v_kernel(tc, x, h, W_ih, W_hh, b_ih, b_hh, gates, h_n,
                     start=(a == 0),
                     stop=(a == PARTS - 1),
                 )
-            return acc
 
         def store(j):
             n, i = chunks[j]
@@ -216,7 +214,8 @@ def tile_blockdiagonalgru_v_kernel(tc, x, h, W_ih, W_hh, b_ih, b_hh, gates, h_n,
                 d_codes, d_scales = quantise(j - 1)
                 for which in weights_of_step(j - 2):
                     quantise_weights(which)
-                acc = multiply(j - 1, d_codes, d_scales)
+                acc = sums.tile([P, BLOCK], F32)
+                multiply(j - 1, acc, d_codes, d_scales, (R, Z))
             if j < steps:
                 d_n = pairs.tile([P, P, PACK], F32)
                 nc.vector.scalar_tensor_tensor(
@@ -239,6 +238,9 @@ def tile_blockdiagonalgru_v_kernel(tc, x, h, W_ih, W_hh, b_ih, b_hh, gates, h_n,
                 )
                 if nxt < steps:
                     turn(nxt, "r_hn", factors[nxt][1], ident_f32)
+            if j > 0:
+                multiply(j - 1, acc, d_codes, d_scales, (N,))
+            if j < steps:
                 nc.vector.tensor_tensor(out=dgi[:, Z], in0=words(j, "c_minus_h"), in1=minus_az[:], op=ALU.mult)
                 if nxt < steps:
                     turn_c_minus_h(nxt)

@@ -38,7 +38,8 @@ def tile_blockdiagonalgru_v_kernel(tc, x, h, W_ih, W_hh, b_ih, b_hh, gates, h_n,
         loads = ctx.enter_context(tc.tile_pool(name="loads", bufs=LOAD_AHEAD))
         w_raws = ctx.enter_context(tc.tile_pool(name="w_raws", bufs=4))
         pairs = ctx.enter_context(tc.tile_pool(name="pairs", bufs=2))
-        w_groups = ctx.enter_context(tc.tile_pool(name="w_groups", bufs=PARTS))
+        triples = ctx.enter_context(tc.tile_pool(name="triples", bufs=3))
+        w_groups = ctx.enter_context(tc.tile_pool(name="w_groups", bufs=PARTS + 1))
         banks = ctx.enter_context(tc.psum_pool(name="banks", bufs=1))
         sums = ctx.enter_context(tc.psum_pool(name="sums", bufs=2))
         ctx.enter_context(tc.manual_schedule())
@@ -61,10 +62,10 @@ def tile_blockdiagonalgru_v_kernel(tc, x, h, W_ih, W_hh, b_ih, b_hh, gates, h_n,
         w_grouped_of = {}
 
         def weights_of_step(step):
-            if step == -1:
+            if step == 0:
                 return [(0, a) for a in range(PARTS)]
-            n, a = step // ROW_TILES + 1, step % ROW_TILES
-            return [(n, a)] if (step >= 0 and n < BLOCKS and a < PARTS) else []
+            n, a = step // ROW_TILES + 1, step % ROW_TILES - 1
+            return [(n, a)] if (step > 0 and n < BLOCKS and a >= 0) else []
 
         def load_weights(which):
             n, a = which
@@ -152,8 +153,8 @@ def tile_blockdiagonalgru_v_kernel(tc, x, h, W_ih, W_hh, b_ih, b_hh, gates, h_n,
 
         def quantise(j):
             dgi = rounded[j]
-            d_codes = pairs.tile([P, PARTS, P], U32, align_bytes=64)
-            d_scales = pairs.tile([P, PARTS, P], U8, align_bytes=64)
+            d_codes = triples.tile([P, PARTS, P], U32, align_bytes=64)
+            d_scales = triples.tile([P, PARTS, P], U8, align_bytes=64)
             nc.vector.quantize_mx(
                 out=d_codes[:, R : Z + 1, :].rearrange("p a b -> p (a b)").bitcast(E5M2_X4),
                 scales=d_scales[:, R : Z + 1, :].rearrange("p a b -> p (a b)"),
@@ -166,9 +167,11 @@ def tile_blockdiagonalgru_v_kernel(tc, x, h, W_ih, W_hh, b_ih, b_hh, gates, h_n,
             )
             return d_codes, d_scales
 
-        def multiply(j, acc, d_codes, d_scales, parts):
+        def multiply(j, words_and_scales):
             n, i = chunks[j]
-            for a in parts:
+            d_codes, d_scales = words_and_scales
+            acc = sums.tile([P, BLOCK], F32)
+            for a in range(PARTS):
                 nc.tensor.matmul_mx(
                     out=acc[:],
                     lhsT=d_codes[:, a, :].bitcast(E5M2_X4),
@@ -178,6 +181,7 @@ def tile_blockdiagonalgru_v_kernel(tc, x, h, W_ih, W_hh, b_ih, b_hh, gates, h_n,
                     start=(a == 0),
                     stop=(a == PARTS - 1),
                 )
+            return acc
 
         def store(j):
             n, i = chunks[j]
@@ -192,12 +196,11 @@ def tile_blockdiagonalgru_v_kernel(tc, x, h, W_ih, W_hh, b_ih, b_hh, gates, h_n,
         turn(0, "r_hn", factors[0][1], ident_f32)
         turn_c_minus_h(0)
         turn(0, "r", loaded[0][1][:, GATE_R, :], ident_f32)
-        for which in weights_of_step(-1):
-            regroup_weights(which)
         make_factors(1)
 
         first_step_without_loads = steps - LOAD_AHEAD
-        for j in range(steps + 1):
+        quantised = {}
+        for j in range(steps + 2):
             nxt = j + 1
             stream_in(j + LOAD_AHEAD)
             turn_g(nxt)
@@ -210,12 +213,12 @@ def tile_blockdiagonalgru_v_kernel(tc, x, h, W_ih, W_hh, b_ih, b_hh, gates, h_n,
                     out=minus_a[:], in0=z_words, scalar=1.0, in1=turned[(j, "g")][:],
                     op0=ALU.subtract, op1=ALU.mult,
                 )
-            if j > 0:
-                d_codes, d_scales = quantise(j - 1)
-                for which in weights_of_step(j - 2):
-                    quantise_weights(which)
-                acc = sums.tile([P, BLOCK], F32)
-                multiply(j - 1, acc, d_codes, d_scales, (R, Z))
+            if 0 <= j - 1 < steps:
+                quantised[j - 1] = quantise(j - 1)
+            for which in weights_of_step(j - 2):
+                quantise_weights(which)
+            if j >= 2:
+                acc = multiply(j - 2, quantised[j - 2])
             if j < steps:
                 d_n = pairs.tile([P, P, PACK], F32)
                 nc.vector.scalar_tensor_tensor(
@@ -238,9 +241,6 @@ def tile_blockdiagonalgru_v_kernel(tc, x, h, W_ih, W_hh, b_ih, b_hh, gates, h_n,
                 )
                 if nxt < steps:
                     turn(nxt, "r_hn", factors[nxt][1], ident_f32)
-            if j > 0:
-                multiply(j - 1, acc, d_codes, d_scales, (N,))
-            if j < steps:
                 nc.vector.tensor_tensor(out=dgi[:, Z], in0=words(j, "c_minus_h"), in1=minus_az[:], op=ALU.mult)
                 if nxt < steps:
                     turn_c_minus_h(nxt)
@@ -252,11 +252,11 @@ def tile_blockdiagonalgru_v_kernel(tc, x, h, W_ih, W_hh, b_ih, b_hh, gates, h_n,
                     turn(nxt, "r", loaded[nxt][1][:, GATE_R, :], ident_f32)
             for which in weights_of_step(j):
                 regroup_weights(which)
-            if j > 0:
-                nc.scalar.copy(out=results[:, j - 1, :], in_=acc[:])
+            if j >= 2:
+                nc.scalar.copy(out=results[:, j - 2, :], in_=acc[:])
             if j == first_step_without_loads:
-                for finished in range(j - 1):
+                for finished in range(j - 2):
                     store(finished)
             if j >= first_step_without_loads:
-                store(j - 1)
+                store(j - 2)
             make_factors(j + 2)

from contextlib import ExitStack

import concourse.mybir as mybir
from concourse.masks import make_identity

F32 = mybir.dt.float32
BF16 = mybir.dt.bfloat16
U32 = mybir.dt.uint32
U8 = mybir.dt.uint8
E4M3_X4 = mybir.dt.float8_e4m3fn_x4
E5M2_X4 = mybir.dt.float8_e5m2_x4
ALU = mybir.AluOpType
ACT = mybir.ActivationFunctionType

P = 128
PACK = 4
BATCH = 512
BLOCKS = 4
BLOCK = 512
PARTS = 3
ROW_TILES = BATCH // P
R, Z, N = 0, 1, 2
GATE_R, GATE_Z, GATE_C = 0, 1, 2

LOAD_AHEAD = 5

FLOPS = 2 * BATCH * BLOCKS * PARTS * BLOCK * BLOCK
BYTES = BATCH * BLOCKS * BLOCK * (PARTS * 4 + 4 + 2 + 2 + 4) + BLOCKS * PARTS * BLOCK * BLOCK * 2


def tile_blockdiagonalgru_v_kernel(tc, x, h, W_ih, W_hh, b_ih, b_hh, gates, h_n, grad_out, out):
    nc = tc.nc
    chunks = [(n, i) for n in range(BLOCKS) for i in range(ROW_TILES)]
    steps = len(chunks)

    with ExitStack() as ctx:
        keep = ctx.enter_context(tc.tile_pool(name="keep", bufs=1))
        loads = ctx.enter_context(tc.tile_pool(name="loads", bufs=LOAD_AHEAD))
        w_raws = ctx.enter_context(tc.tile_pool(name="w_raws", bufs=4))
        pairs = ctx.enter_context(tc.tile_pool(name="pairs", bufs=2))
        triples = ctx.enter_context(tc.tile_pool(name="triples", bufs=3))
        w_groups = ctx.enter_context(tc.tile_pool(name="w_groups", bufs=PARTS + 1))
        banks = ctx.enter_context(tc.psum_pool(name="banks", bufs=1))
        sums = ctx.enter_context(tc.psum_pool(name="sums", bufs=2))
        ctx.enter_context(tc.manual_schedule())

        ident_f32 = keep.tile([P, P], F32)
        make_identity(nc, ident_f32[:])
        ident_bf16 = keep.tile([P, P], BF16)
        make_identity(nc, ident_bf16[:])
        minus_ident_bf16 = keep.tile([P, P], BF16)
        nc.vector.tensor_scalar_mul(out=minus_ident_bf16[:], in0=ident_bf16[:], scalar1=-1.0)
        w_codes = keep.tile([P, BLOCKS, PARTS, BLOCK], U32, align_bytes=64)
        w_scales = keep.tile([P, BLOCKS, PARTS, BLOCK], U8, align_bytes=64)
        results = keep.tile([P, steps, BLOCK], F32)

        loaded = {}
        factors = {}
        turned = {}
        rounded = {}
        w_raw_of = {}
        w_grouped_of = {}

        def weights_of_step(step):
            if step == 0:
                return [(0, a) for a in range(PARTS)]
            n, a = step // ROW_TILES + 1, step % ROW_TILES - 1
            return [(n, a)] if (step > 0 and n < BLOCKS and a >= 0) else []

        def load_weights(which):
            n, a = which
            w_raw = w_raws.tile([P, PACK, BLOCK], BF16)
            rows = W_ih[n, a * BLOCK : (a + 1) * BLOCK, :]
            nc.sync.dma_start(out=w_raw[:], in_=rows.rearrange("(t p) j -> p t j", p=P))
            w_raw_of[which] = w_raw

        def regroup_weights(which):
            w_grouped = w_groups.tile([P, BLOCK, PACK], BF16, align_bytes=64)
            nc.scalar.copy(
                out=w_grouped[:].rearrange("p (c i) t -> p c t i", i=4),
                in_=w_raw_of[which][:].rearrange("p t (c i) -> p c t i", i=4),
            )
            w_grouped_of[which] = w_grouped

        def quantise_weights(which):
            n, a = which
            nc.vector.quantize_mx(
                out=w_codes[:, n, a, :].bitcast(E4M3_X4),
                scales=w_scales[:, n, a, :],
                in_=w_grouped_of[which][:].rearrange("p j t -> p (j t)"),
            )

        def load_chunk(j):
            n, i = chunks[j]
            rows = slice(i * P, (i + 1) * P)
            cols = slice(n * BLOCK, (n + 1) * BLOCK)
            g_in = loads.tile([P, BLOCK], BF16)
            nc.sync.dma_start(out=g_in[:], in_=grad_out[rows, cols])
            gates_in = loads.tile([P, PARTS, BLOCK], F32)
            nc.sync.dma_start(out=gates_in[:], in_=gates[rows, n, :].rearrange("b (a k) -> b a k", a=PARTS))
            h_in = loads.tile([P, BLOCK], BF16)
            nc.sync.dma_start(out=h_in[:], in_=h[rows, cols])
            hn_in = loads.tile([P, BLOCK], F32)
            nc.sync.dma_start(out=hn_in[:], in_=h_n[rows, n, :])
            loaded[j] = (g_in, gates_in, h_in, hn_in)

        def stream_in(j):
            for which in weights_of_step(j - 2):
                load_weights(which)
            if j < steps:
                load_chunk(j)

        def make_factors(j):
            if j >= steps:
                return
            g_in, gates_in, h_in, hn_in = loaded[j]
            c_sq = pairs.tile([P, BLOCK], F32)
            nc.scalar.activation(out=c_sq[:], in_=gates_in[:, GATE_C, :], func=ACT.Square)
            r_hn = pairs.tile([P, BLOCK], F32)
            nc.gpsimd.tensor_tensor(out=r_hn[:], in0=gates_in[:, GATE_R, :], in1=hn_in[:], op=ALU.mult)
            factors[j] = (c_sq, r_hn)

        def turn(j, name, plane, identity):
            bank = banks.tile([P, PACK, P], plane.dtype, name=name)
            for t in range(PACK):
                nc.tensor.transpose(out=bank[:, t, :], in_=plane[:, t * P : (t + 1) * P], identity=identity[:])
            turned[(j, name)] = bank

        def turn_c_minus_h(j):
            g_in, gates_in, h_in, hn_in = loaded[j]
            bank = banks.tile([P, PACK, P], F32, name="c_minus_h")
            for t in range(PACK):
                k = slice(t * P, (t + 1) * P)
                nc.tensor.matmul(
                    out=bank[:, t, :], lhsT=gates_in[:, GATE_C, k], rhs=ident_f32[:],
                    is_transpose=True, start=True, stop=False,
                )
                nc.tensor.matmul(
                    out=bank[:, t, :], lhsT=h_in[:, k], rhs=minus_ident_bf16[:], start=False, stop=True
                )
            turned[(j, "c_minus_h")] = bank

        def words(j, name):
            return turned[(j, name)][:].rearrange("p t b -> p b t")

        def turn_g(j):
            if j >= steps:
                return
            turn(j, "g_bank", loaded[j][0], ident_bf16)
            g_t = pairs.tile([P, P, PACK], BF16)
            nc.scalar.copy(out=g_t[:], in_=words(j, "g_bank"))
            turned[(j, "g")] = g_t

        def quantise(j):
            dgi = rounded[j]
            d_codes = triples.tile([P, PARTS, P], U32, align_bytes=64)
            d_scales = triples.tile([P, PARTS, P], U8, align_bytes=64)
            nc.vector.quantize_mx(
                out=d_codes[:, R : Z + 1, :].rearrange("p a b -> p (a b)").bitcast(E5M2_X4),
                scales=d_scales[:, R : Z + 1, :].rearrange("p a b -> p (a b)"),
                in_=dgi[:, R : Z + 1].rearrange("p a b t -> p (a b t)"),
            )
            nc.vector.quantize_mx(
                out=d_codes[:, N, :].bitcast(E5M2_X4),
                scales=d_scales[:, N, :],
                in_=dgi[:, N].rearrange("p b t -> p (b t)"),
            )
            return d_codes, d_scales

        def multiply(j, words_and_scales):
            n, i = chunks[j]
            d_codes, d_scales = words_and_scales
            acc = sums.tile([P, BLOCK], F32)
            for a in range(PARTS):
                nc.tensor.matmul_mx(
                    out=acc[:],
                    lhsT=d_codes[:, a, :].bitcast(E5M2_X4),
                    lhsT_scale=d_scales[:, a, :],
                    rhs=w_codes[:, n, a, :].bitcast(E4M3_X4),
                    rhs_scale=w_scales[:, n, a, :],
                    start=(a == 0),
                    stop=(a == PARTS - 1),
                )
            return acc

        def store(j):
            n, i = chunks[j]
            nc.sync.dma_start(out=out[i * P : (i + 1) * P, n * BLOCK : (n + 1) * BLOCK], in_=results[:, j, :])

        for j in range(LOAD_AHEAD):
            stream_in(j)
        make_factors(0)
        turn_g(0)
        turn(0, "c_sq", factors[0][0], ident_f32)
        turn(0, "z", loaded[0][1][:, GATE_Z, :], ident_f32)
        turn(0, "r_hn", factors[0][1], ident_f32)
        turn_c_minus_h(0)
        turn(0, "r", loaded[0][1][:, GATE_R, :], ident_f32)
        make_factors(1)

        first_step_without_loads = steps - LOAD_AHEAD
        quantised = {}
        for j in range(steps + 2):
            nxt = j + 1
            stream_in(j + LOAD_AHEAD)
            turn_g(nxt)
            if j < steps:
                dgi = pairs.tile([P, PARTS, P, PACK], BF16, align_bytes=64)
                rounded[j] = dgi
                z_words = words(j, "z")
                minus_a = pairs.tile([P, P, PACK], F32)
                nc.vector.scalar_tensor_tensor(
                    out=minus_a[:], in0=z_words, scalar=1.0, in1=turned[(j, "g")][:],
                    op0=ALU.subtract, op1=ALU.mult,
                )
            if 0 <= j - 1 < steps:
                quantised[j - 1] = quantise(j - 1)
            for which in weights_of_step(j - 2):
                quantise_weights(which)
            if j >= 2:
                acc = multiply(j - 2, quantised[j - 2])
            if j < steps:
                d_n = pairs.tile([P, P, PACK], F32)
                nc.vector.scalar_tensor_tensor(
                    out=d_n[:], in0=words(j, "c_sq"), scalar=1.0, in1=minus_a[:],
                    op0=ALU.subtract, op1=ALU.mult,
                )
                if nxt < steps:
                    turn(nxt, "c_sq", factors[nxt][0], ident_f32)
                nc.gpsimd.tensor_scalar(
                    out=dgi[:, N], in0=d_n[:], scalar1=1.0, scalar2=0.0, op0=ALU.mult, op1=ALU.add
                )
                minus_az = pairs.tile([P, P, PACK], F32)
                nc.vector.tensor_tensor(out=minus_az[:], in0=z_words, in1=minus_a[:], op=ALU.mult)
                if nxt < steps:
                    turn(nxt, "z", loaded[nxt][1][:, GATE_Z, :], ident_f32)
                minus_dn_r_hn = pairs.tile([P, P, PACK], F32)
                nc.vector.scalar_tensor_tensor(
                    out=minus_dn_r_hn[:], in0=words(j, "r_hn"), scalar=-1.0, in1=d_n[:],
                    op0=ALU.mult, op1=ALU.mult,
                )
                if nxt < steps:
                    turn(nxt, "r_hn", factors[nxt][1], ident_f32)
                nc.vector.tensor_tensor(out=dgi[:, Z], in0=words(j, "c_minus_h"), in1=minus_az[:], op=ALU.mult)
                if nxt < steps:
                    turn_c_minus_h(nxt)
                nc.vector.scalar_tensor_tensor(
                    out=dgi[:, R], in0=words(j, "r"), scalar=1.0, in1=minus_dn_r_hn[:],
                    op0=ALU.subtract, op1=ALU.mult,
                )
                if nxt < steps:
                    turn(nxt, "r", loaded[nxt][1][:, GATE_R, :], ident_f32)
            for which in weights_of_step(j):
                regroup_weights(which)
            if j >= 2:
                nc.scalar.copy(out=results[:, j - 2, :], in_=acc[:])
            if j == first_step_without_loads:
                for finished in range(j - 2):
                    store(finished)
            if j >= first_step_without_loads:
                store(j - 2)
            make_factors(j + 2)
